import numpy as np
import ml_dtypes


def mxq(x, axis, fmt="e4m3"):
    dtype, down = {"e4m3": (ml_dtypes.float8_e4m3fn, 7), "e5m2": (ml_dtypes.float8_e5m2, 14)}[fmt]
    v = np.moveaxis(np.asarray(x, np.float32).astype(ml_dtypes.bfloat16).astype(np.float64), axis, -1)
    blocks = v.reshape(v.shape[:-1] + (-1, 32))
    amax = np.abs(blocks).max(-1, keepdims=True)
    byte = np.maximum(np.where(amax > 0, np.frexp(amax)[1] - 1 + 127, 0) - down, 1)
    scale = np.exp2(byte - 127.0)
    codes = (blocks / scale).astype(np.float32).astype(dtype).astype(np.float64)
    return np.moveaxis((codes * scale).reshape(v.shape), -1, axis)


WIDE = False


def mx_kscale(k):
    if not WIDE:
        return np.ones(k)
    levels = np.array([10, -10, 5, -5, 0])
    a = np.random.permutation(np.resize(levels, k // 512 * 4)).reshape(k // 512, 4)
    idx = np.arange(k)
    return np.exp2(a[idx // 512, idx % 128 // 32])


BF16 = ml_dtypes.bfloat16


def bf(x):
    return np.asarray(x, np.float32).astype(BF16)


def f64(x):
    return np.asarray(x).astype(np.float64)


B, S, SV, H, DH = 1, 16384, 1024, 8, 64
SCALE = DH ** (-0.5)


def _flatten_like_module(t):
    b, s, h, dh = t.shape
    return np.transpose(t, (0, 2, 1, 3)).reshape(b, s, h * dh)


def _heads_to_batch(t):
    b, s, d = t.shape
    t = t.reshape(b, s, H, d // H)
    t = np.transpose(t, (0, 2, 1, 3))
    return t.reshape(b * H, s, d // H)


def setup_inputs():
    a = np.sqrt(2.0 / (SCALE * np.sqrt(S)))
    sc = mx_kscale(S)
    f = np.repeat(sc.reshape(H, S // H).T, H, axis=0)[None, :, :, None]
    return {"query": bf(np.random.standard_normal((B, S, H, DH)) * a * f),
            "key": bf(np.random.standard_normal((B, S, H, DH)) * a / f),
            "value": bf(np.random.standard_normal((B, SV, H, DH)))}


def reference(query, key, value):
    q = _heads_to_batch(_flatten_like_module(f64(query)))
    k = _heads_to_batch(_flatten_like_module(f64(key)))
    scores = (mxq(q, 1, "e4m3").transpose(0, 2, 1) @ mxq(k, 1, "e4m3")) * SCALE
    e = np.exp(scores - scores.max(axis=2, keepdims=True))
    return e / e.sum(axis=2, keepdims=True)

@@ -1,0 +1,170 @@
+from contextlib import ExitStack
+
+import concourse.mybir as mybir
+
+BF16 = mybir.dt.bfloat16
+F32 = mybir.dt.float32
+U32 = mybir.dt.uint32
+U8 = mybir.dt.uint8
+FP8X4 = mybir.dt.float8_e4m3fn_x4
+EXP = mybir.ActivationFunctionType.Exp
+AX = mybir.AxisListType.X
+
+P = 128
+PACK = 4
+S = 16384
+H = 8
+DH = 64
+G = 8
+CB = 4
+UNIT = H * DH
+SCALE = 0.125
+GC = 4
+RAW_BUFS = 8
+
+FLOPS = 2 * G * DH * DH * S
+BYTES = 2 * S * H * DH * 2 + G * DH * DH * 4
+
+
+def tile_flaxattention2_kernel(tc, query, key, value, out):
+    nc = tc.nc
+    pattern = "b (c p t g) h d -> (b c) p t (g h d)"
+    views = [x.rearrange(pattern, c=CB, p=P, t=PACK, g=G) for x in (query, key)]
+    out_rows = out.rearrange("g d e -> (g d) e")
+
+    chunks = [(ten, c, part) for c in range(CB) for part in range(G // GC) for ten in range(2)]
+    steps = []
+    for k, (ten, c, part) in enumerate(chunks):
+        for pl in range(GC // 2):
+            steps.append((ten, c, part * (GC // 2) + pl, k, pl))
+    n_steps = len(steps)
+
+    with ExitStack() as ctx:
+        raw_pool = ctx.enter_context(tc.tile_pool(name="raw", bufs=RAW_BUFS))
+        grp_pool = ctx.enter_context(tc.tile_pool(name="grp", bufs=3))
+        wrd_pool = ctx.enter_context(tc.tile_pool(name="wrd", bufs=6))
+        small = ctx.enter_context(tc.tile_pool(name="small", bufs=1))
+        soft = ctx.enter_context(tc.tile_pool(name="soft", bufs=4))
+        psum = ctx.enter_context(tc.psum_pool(name="acc", bufs=1))
+        ctx.enter_context(tc.manual_schedule())
+
+        acc = [psum.tile([P, 2 * DH], F32, name="acc%d" % gp) for gp in range(G // 2)]
+        raws = {}
+        grouped = {}
+        words = {}
+        planes = {}
+        soft_tiles = {}
+
+        def load(k):
+            ten, c, part = chunks[k]
+            raw = raw_pool.tile([P, PACK, GC * UNIT], BF16, name="raw")
+            nc.sync.dma_start(out=raw[:], in_=views[ten][c][:, :, part * GC * UNIT : (part + 1) * GC * UNIT])
+            raws[k] = raw
+
+        def regroup(u):
+            ten, c, gp, k, pl = steps[u]
+            grp = grp_pool.tile([P, H, 2, DH, PACK], BF16, name="grp", align_bytes=64)
+            grouped[u] = grp
+            for g2, copy in ((0, nc.vector.tensor_copy), (1, nc.scalar.copy)):
+                gl = 2 * pl + g2
+                src = raws[k][:, :, gl * UNIT : (gl + 1) * UNIT].rearrange("p t (h c i) -> p h c t i", h=H, i=4)
+                dst = grp[:, :, g2, :, :].rearrange("p h (c i) t -> p h c t i", i=4)
+                copy(out=dst, in_=src)
+
+        def quantise(u):
+            wrd = wrd_pool.tile([P, 2 * UNIT], U32, name="wrd", align_bytes=64)
+            pln = wrd_pool.tile([P, 2 * UNIT], U8, name="pln", align_bytes=64)
+            nc.vector.quantize_mx(
+                out=wrd[:].bitcast(FP8X4),
+                scales=pln[:],
+                in_=grouped[u][:].rearrange("p h g d t -> p (h g d t)"),
+            )
+            words[u] = wrd
+            planes[u] = pln
+
+        def multiply(uq, uk):
+            ten, c, gp, k, pl = steps[uk]
+            for h in range(H):
+                cols = slice(2 * DH * h, 2 * DH * (h + 1))
+                nc.tensor.matmul_mx(
+                    out=acc[gp][:],
+                    lhsT=words[uq][:, cols].bitcast(FP8X4),
+                    lhsT_scale=planes[uq][:, cols],
+                    rhs=words[uk][:, cols].bitcast(FP8X4),
+                    rhs_scale=planes[uk][:, cols],
+                    start=(c == 0 and h == 0),
+                    stop=(c == CB - 1 and h == H - 1),
+                )
+
+        def soft_max(gp):
+            top = soft.tile([P, 1], F32, name="top")
+            shift = soft.tile([P, 1], F32, name="shift")
+            for g2 in range(2):
+                rows = slice(DH * g2, DH * (g2 + 1))
+                nc.vector.reduce_max(out=top[rows, :], in_=acc[gp][rows, rows], axis=AX)
+            nc.vector.tensor_scalar_mul(out=shift[:], in0=top[:], scalar1=-SCALE)
+            soft_tiles[gp] = [shift]
+
+        def soft_exp(gp):
+            shift = soft_tiles[gp][0]
+            expo = soft.tile([P, DH], F32, name="expo")
+            total = soft.tile([P, 1], F32, name="total")
+            for g2 in range(2):
+                rows = slice(DH * g2, DH * (g2 + 1))
+                nc.scalar.activation(
+                    out=expo[rows, :],
+                    in_=acc[gp][rows, rows],
+                    func=EXP,
+                    bias=shift[rows, :],
+                    scale=SCALE,
+                    accum_out=total[rows, :],
+                )
+            soft_tiles[gp] = [expo, total]
+
+        def soft_norm(gp):
+            expo, total = soft_tiles[gp]
+            inv = soft.tile([P, 1], F32, name="inv")
+            prob = soft.tile([P, DH], F32, name="prob")
+            nc.vector.reciprocal(out=inv[:], in_=total[:])
+            nc.vector.tensor_scalar_mul(out=prob[:], in0=expo[:], scalar1=inv[:, 0:1])
+            nc.sync.dma_start(out=out_rows[P * gp : P * (gp + 1), :], in_=prob[:])
+
+        warm_in = small.tile([P, 1], F32, name="warm_in")
+        warm_out = small.tile([P, 1], F32, name="warm_out")
+        nc.vector.memset(warm_in[:], 0.0)
+        nc.scalar.activation(out=warm_out[:], in_=warm_in[:], func=EXP)
+
+        for k in range(min(RAW_BUFS, len(chunks))):
+            load(k)
+
+        open_q = {}
+        stage_max = {}
+        stage_norm = {}
+        regroup(0)
+        for u in range(n_steps):
+            ten, c, gp, k, pl = steps[u]
+            if u + 1 < n_steps:
+                regroup(u + 1)
+                k_next = steps[u + 1][3]
+                last_of_chunk = u + 2 >= n_steps or steps[u + 2][3] != k_next
+                if last_of_chunk and k_next + RAW_BUFS < len(chunks):
+                    load(k_next + RAW_BUFS)
+            for done in stage_max.get(u, []):
+                soft_max(done)
+                soft_exp(done)
+            quantise(u)
+            if ten == 0:
+                open_q[(c, gp)] = u
+            else:
+                multiply(open_q[(c, gp)], u)
+                if c == CB - 1:
+                    stage_max[u + 1] = [gp]
+                    stage_norm[u + 2] = [gp]
+            for done in stage_norm.get(u, []):
+                soft_norm(done)
+        for u in (n_steps, n_steps + 1):
+            for done in stage_norm.get(u, []):
+                soft_norm(done)
+            for done in stage_max.get(u, []):
+                soft_max(done)
+                soft_exp(done)

@@ -19,8 +19,8 @@ G = 8
 CB = 4
 UNIT = H * DH
 SCALE = 0.125
-GC = 4
-RAW_BUFS = 8
+GC = 2
+RAW_BUFS = 12
 
 FLOPS = 2 * G * DH * DH * S
 BYTES = 2 * S * H * DH * 2 + G * DH * DH * 4
@@ -140,15 +140,19 @@ def tile_flaxattention2_kernel(tc, query, key, value, out):
         open_q = {}
         stage_max = {}
         stage_norm = {}
-        regroup(0)
+
+        def regroup_and_refill(u):
+            regroup(u)
+            k_now = steps[u][3]
+            last_of_chunk = u + 1 >= n_steps or steps[u + 1][3] != k_now
+            if last_of_chunk and k_now + RAW_BUFS < len(chunks):
+                load(k_now + RAW_BUFS)
+
+        regroup_and_refill(0)
         for u in range(n_steps):
             ten, c, gp, k, pl = steps[u]
             if u + 1 < n_steps:
-                regroup(u + 1)
-                k_next = steps[u + 1][3]
-                last_of_chunk = u + 2 >= n_steps or steps[u + 2][3] != k_next
-                if last_of_chunk and k_next + RAW_BUFS < len(chunks):
-                    load(k_next + RAW_BUFS)
+                regroup_and_refill(u + 1)
             for done in stage_max.get(u, []):
                 soft_max(done)
                 soft_exp(done)

@@ -19,8 +19,9 @@ G = 8
 CB = 4
 UNIT = H * DH
 SCALE = 0.125
-GC = 2
-RAW_BUFS = 12
+GC = 4
+RAW_BUFS = 8
+VECTOR_BOTH = (10, 21)
 
 FLOPS = 2 * G * DH * DH * S
 BYTES = 2 * S * H * DH * 2 + G * DH * DH * 4
@@ -65,7 +66,8 @@ def tile_flaxattention2_kernel(tc, query, key, value, out):
             ten, c, gp, k, pl = steps[u]
             grp = grp_pool.tile([P, H, 2, DH, PACK], BF16, name="grp", align_bytes=64)
             grouped[u] = grp
-            for g2, copy in ((0, nc.vector.tensor_copy), (1, nc.scalar.copy)):
+            for g2 in range(2):
+                copy = nc.vector.tensor_copy if (g2 == 0 or u in VECTOR_BOTH) else nc.scalar.copy
                 gl = 2 * pl + g2
                 src = raws[k][:, :, gl * UNIT : (gl + 1) * UNIT].rearrange("p t (h c i) -> p h c t i", h=H, i=4)
                 dst = grp[:, :, g2, :, :].rearrange("p h (c i) t -> p h c t i", i=4)

@@ -20,8 +20,10 @@ CB = 4
 UNIT = H * DH
 SCALE = 0.125
 GC = 4
+PAIRS = GC // 2
 RAW_BUFS = 8
-VECTOR_BOTH = (10, 21)
+FINE_HEAD = 2
+FINE_TAIL = 2
 
 FLOPS = 2 * G * DH * DH * S
 BYTES = 2 * S * H * DH * 2 + G * DH * DH * 4
@@ -34,11 +36,15 @@ def tile_flaxattention2_kernel(tc, query, key, value, out):
     out_rows = out.rearrange("g d e -> (g d) e")
 
     chunks = [(ten, c, part) for c in range(CB) for part in range(G // GC) for ten in range(2)]
-    steps = []
-    for k, (ten, c, part) in enumerate(chunks):
-        for pl in range(GC // 2):
-            steps.append((ten, c, part * (GC // 2) + pl, k, pl))
-    n_steps = len(steps)
+    n_chunks = len(chunks)
+    groups = []
+    for k in range(n_chunks):
+        if k < FINE_HEAD or k >= n_chunks - FINE_TAIL:
+            for pl in range(PAIRS):
+                groups.append((k, pl, 1))
+        else:
+            groups.append((k, 0, PAIRS))
+    n_groups = len(groups)
 
     with ExitStack() as ctx:
         raw_pool = ctx.enter_context(tc.tile_pool(name="raw", bufs=RAW_BUFS))
@@ -62,38 +68,40 @@ def tile_flaxattention2_kernel(tc, query, key, value, out):
             nc.sync.dma_start(out=raw[:], in_=views[ten][c][:, :, part * GC * UNIT : (part + 1) * GC * UNIT])
             raws[k] = raw
 
-        def regroup(u):
-            ten, c, gp, k, pl = steps[u]
-            grp = grp_pool.tile([P, H, 2, DH, PACK], BF16, name="grp", align_bytes=64)
-            grouped[u] = grp
-            for g2 in range(2):
-                copy = nc.vector.tensor_copy if (g2 == 0 or u in VECTOR_BOTH) else nc.scalar.copy
-                gl = 2 * pl + g2
-                src = raws[k][:, :, gl * UNIT : (gl + 1) * UNIT].rearrange("p t (h c i) -> p h c t i", h=H, i=4)
-                dst = grp[:, :, g2, :, :].rearrange("p h (c i) t -> p h c t i", i=4)
+        def regroup(n):
+            k, pl0, npl = groups[n]
+            grp = grp_pool.tile([P, PAIRS, H, 2, DH, PACK], BF16, name="grp", align_bytes=64)
+            grouped[n] = grp
+            src_all = raws[k][:].rearrange("p t (l g h c i) -> p l g h c t i", l=PAIRS, g=2, h=H, i=4)
+            for g2, copy in ((0, nc.vector.tensor_copy), (1, nc.scalar.copy)):
+                src = src_all[:, pl0 : pl0 + npl, g2, :, :, :, :]
+                dst = grp[:, 0:npl, :, g2, :, :].rearrange("p l h (c i) t -> p l h c t i", i=4)
                 copy(out=dst, in_=src)
+            if pl0 + npl == PAIRS and k + RAW_BUFS < n_chunks:
+                load(k + RAW_BUFS)
 
-        def quantise(u):
+        def quantise(n, l):
+            k, pl0, npl = groups[n]
             wrd = wrd_pool.tile([P, 2 * UNIT], U32, name="wrd", align_bytes=64)
             pln = wrd_pool.tile([P, 2 * UNIT], U8, name="pln", align_bytes=64)
             nc.vector.quantize_mx(
                 out=wrd[:].bitcast(FP8X4),
                 scales=pln[:],
-                in_=grouped[u][:].rearrange("p h g d t -> p (h g d t)"),
+                in_=grouped[n][:, l, :, :, :, :].rearrange("p h g d t -> p (h g d t)"),
             )
-            words[u] = wrd
-            planes[u] = pln
+            ten, c, part = chunks[k]
+            words[(ten, c, part * PAIRS + pl0 + l)] = wrd
+            planes[(ten, c, part * PAIRS + pl0 + l)] = pln
 
-        def multiply(uq, uk):
-            ten, c, gp, k, pl = steps[uk]
+        def multiply(c, gp):
             for h in range(H):
                 cols = slice(2 * DH * h, 2 * DH * (h + 1))
                 nc.tensor.matmul_mx(
                     out=acc[gp][:],
-                    lhsT=words[uq][:, cols].bitcast(FP8X4),
-                    lhsT_scale=planes[uq][:, cols],
-                    rhs=words[uk][:, cols].bitcast(FP8X4),
-                    rhs_scale=planes[uk][:, cols],
+                    lhsT=words[(0, c, gp)][:, cols].bitcast(FP8X4),
+                    lhsT_scale=planes[(0, c, gp)][:, cols],
+                    rhs=words[(1, c, gp)][:, cols].bitcast(FP8X4),
+                    rhs_scale=planes[(1, c, gp)][:, cols],
                     start=(c == 0 and h == 0),
                     stop=(c == CB - 1 and h == H - 1),
                 )
@@ -136,41 +144,33 @@ def tile_flaxattention2_kernel(tc, query, key, value, out):
         nc.vector.memset(warm_in[:], 0.0)
         nc.scalar.activation(out=warm_out[:], in_=warm_in[:], func=EXP)
 
-        for k in range(min(RAW_BUFS, len(chunks))):
+        for k in range(min(RAW_BUFS, n_chunks)):
             load(k)
 
-        open_q = {}
         stage_max = {}
         stage_norm = {}
-
-        def regroup_and_refill(u):
-            regroup(u)
-            k_now = steps[u][3]
-            last_of_chunk = u + 1 >= n_steps or steps[u + 1][3] != k_now
-            if last_of_chunk and k_now + RAW_BUFS < len(chunks):
-                load(k_now + RAW_BUFS)
-
-        regroup_and_refill(0)
-        for u in range(n_steps):
-            ten, c, gp, k, pl = steps[u]
-            if u + 1 < n_steps:
-                regroup_and_refill(u + 1)
-            for done in stage_max.get(u, []):
+        regroup(0)
+        for n in range(n_groups):
+            k, pl0, npl = groups[n]
+            ten, c, part = chunks[k]
+            if n + 1 < n_groups:
+                regroup(n + 1)
+            for done in stage_max.get(n, []):
                 soft_max(done)
                 soft_exp(done)
-            quantise(u)
-            if ten == 0:
-                open_q[(c, gp)] = u
-            else:
-                multiply(open_q[(c, gp)], u)
-                if c == CB - 1:
-                    stage_max[u + 1] = [gp]
-                    stage_norm[u + 2] = [gp]
-            for done in stage_norm.get(u, []):
+            for l in range(npl):
+                quantise(n, l)
+                if ten == 1:
+                    gp = part * PAIRS + pl0 + l
+                    multiply(c, gp)
+                    if c == CB - 1:
+                        stage_max[n + 1] = stage_max.get(n + 1, []) + [gp]
+                        stage_norm[n + 2] = stage_norm.get(n + 2, []) + [gp]
+            for done in stage_norm.get(n, []):
                 soft_norm(done)
-        for u in (n_steps, n_steps + 1):
-            for done in stage_norm.get(u, []):
+        for n in (n_groups, n_groups + 1):
+            for done in stage_norm.get(n, []):
                 soft_norm(done)
-            for done in stage_max.get(u, []):
+            for done in stage_max.get(n, []):
                 soft_max(done)
                 soft_exp(done)

@@ -20,10 +20,9 @@ CB = 4
 UNIT = H * DH
 SCALE = 0.125
 GC = 4
-PAIRS = GC // 2
 RAW_BUFS = 8
-FINE_HEAD = 2
-FINE_TAIL = 2
+SPLIT_STEPS = 2
+PIECES = 4
 
 FLOPS = 2 * G * DH * DH * S
 BYTES = 2 * S * H * DH * 2 + G * DH * DH * 4
@@ -36,15 +35,11 @@ def tile_flaxattention2_kernel(tc, query, key, value, out):
     out_rows = out.rearrange("g d e -> (g d) e")
 
     chunks = [(ten, c, part) for c in range(CB) for part in range(G // GC) for ten in range(2)]
-    n_chunks = len(chunks)
-    groups = []
-    for k in range(n_chunks):
-        if k < FINE_HEAD or k >= n_chunks - FINE_TAIL:
-            for pl in range(PAIRS):
-                groups.append((k, pl, 1))
-        else:
-            groups.append((k, 0, PAIRS))
-    n_groups = len(groups)
+    steps = []
+    for k, (ten, c, part) in enumerate(chunks):
+        for pl in range(GC // 2):
+            steps.append((ten, c, part * (GC // 2) + pl, k, pl))
+    n_steps = len(steps)
 
     with ExitStack() as ctx:
         raw_pool = ctx.enter_context(tc.tile_pool(name="raw", bufs=RAW_BUFS))
@@ -68,40 +63,37 @@ def tile_flaxattention2_kernel(tc, query, key, value, out):
             nc.sync.dma_start(out=raw[:], in_=views[ten][c][:, :, part * GC * UNIT : (part + 1) * GC * UNIT])
             raws[k] = raw
 
-        def regroup(n):
-            k, pl0, npl = groups[n]
-            grp = grp_pool.tile([P, PAIRS, H, 2, DH, PACK], BF16, name="grp", align_bytes=64)
-            grouped[n] = grp
-            src_all = raws[k][:].rearrange("p t (l g h c i) -> p l g h c t i", l=PAIRS, g=2, h=H, i=4)
+        def regroup(u):
+            ten, c, gp, k, pl = steps[u]
+            grp = grp_pool.tile([P, H, 2, DH, PACK], BF16, name="grp", align_bytes=64)
+            grouped[u] = grp
             for g2, copy in ((0, nc.vector.tensor_copy), (1, nc.scalar.copy)):
-                src = src_all[:, pl0 : pl0 + npl, g2, :, :, :, :]
-                dst = grp[:, 0:npl, :, g2, :, :].rearrange("p l h (c i) t -> p l h c t i", i=4)
+                gl = 2 * pl + g2
+                src = raws[k][:, :, gl * UNIT : (gl + 1) * UNIT].rearrange("p t (h c i) -> p h c t i", h=H, i=4)
+                dst = grp[:, :, g2, :, :].rearrange("p h (c i) t -> p h c t i", i=4)
                 copy(out=dst, in_=src)
-            if pl0 + npl == PAIRS and k + RAW_BUFS < n_chunks:
-                load(k + RAW_BUFS)
 
-        def quantise(n, l):
-            k, pl0, npl = groups[n]
-            wrd = wrd_pool.tile([P, 2 * UNIT], U32, name="wrd", align_bytes=64)
-            pln = wrd_pool.tile([P, 2 * UNIT], U8, name="pln", align_bytes=64)
+        def quantise(u, h0, nh):
+            if h0 == 0:
+                words[u] = wrd_pool.tile([P, 2 * UNIT], U32, name="wrd", align_bytes=64)
+                planes[u] = wrd_pool.tile([P, 2 * UNIT], U8, name="pln", align_bytes=64)
+            cols = slice(2 * DH * h0, 2 * DH * (h0 + nh))
             nc.vector.quantize_mx(
-                out=wrd[:].bitcast(FP8X4),
-                scales=pln[:],
-                in_=grouped[n][:, l, :, :, :, :].rearrange("p h g d t -> p (h g d t)"),
+                out=words[u][:, cols].bitcast(FP8X4),
+                scales=planes[u][:, cols],
+                in_=grouped[u][:, h0 : h0 + nh, :, :, :].rearrange("p h g d t -> p (h g d t)"),
             )
-            ten, c, part = chunks[k]
-            words[(ten, c, part * PAIRS + pl0 + l)] = wrd
-            planes[(ten, c, part * PAIRS + pl0 + l)] = pln
 
-        def multiply(c, gp):
-            for h in range(H):
+        def multiply(uq, uk, h0, nh):
+            ten, c, gp, k, pl = steps[uk]
+            for h in range(h0, h0 + nh):
                 cols = slice(2 * DH * h, 2 * DH * (h + 1))
                 nc.tensor.matmul_mx(
                     out=acc[gp][:],
-                    lhsT=words[(0, c, gp)][:, cols].bitcast(FP8X4),
-                    lhsT_scale=planes[(0, c, gp)][:, cols],
-                    rhs=words[(1, c, gp)][:, cols].bitcast(FP8X4),
-                    rhs_scale=planes[(1, c, gp)][:, cols],
+                    lhsT=words[uq][:, cols].bitcast(FP8X4),
+                    lhsT_scale=planes[uq][:, cols],
+                    rhs=words[uk][:, cols].bitcast(FP8X4),
+                    rhs_scale=planes[uk][:, cols],
                     start=(c == 0 and h == 0),
                     stop=(c == CB - 1 and h == H - 1),
                 )
@@ -144,33 +136,39 @@ def tile_flaxattention2_kernel(tc, query, key, value, out):
         nc.vector.memset(warm_in[:], 0.0)
         nc.scalar.activation(out=warm_out[:], in_=warm_in[:], func=EXP)
 
-        for k in range(min(RAW_BUFS, n_chunks)):
+        for k in range(min(RAW_BUFS, len(chunks))):
             load(k)
 
+        open_q = {}
         stage_max = {}
         stage_norm = {}
         regroup(0)
-        for n in range(n_groups):
-            k, pl0, npl = groups[n]
-            ten, c, part = chunks[k]
-            if n + 1 < n_groups:
-                regroup(n + 1)
-            for done in stage_max.get(n, []):
-                soft_max(done)
-                soft_exp(done)
-            for l in range(npl):
-                quantise(n, l)
+        for u in range(n_steps):
+            ten, c, gp, k, pl = steps[u]
+            if u + 1 < n_steps:
+                regroup(u + 1)
+                k_next = steps[u + 1][3]
+                last_of_chunk = u + 2 >= n_steps or steps[u + 2][3] != k_next
+                if last_of_chunk and k_next + RAW_BUFS < len(chunks):
+                    load(k_next + RAW_BUFS)
+            nh = H // PIECES if u >= n_steps - SPLIT_STEPS else H
+            for h0 in range(0, H, nh):
+                quantise(u, h0, nh)
                 if ten == 1:
-                    gp = part * PAIRS + pl0 + l
-                    multiply(c, gp)
-                    if c == CB - 1:
-                        stage_max[n + 1] = stage_max.get(n + 1, []) + [gp]
-                        stage_norm[n + 2] = stage_norm.get(n + 2, []) + [gp]
-            for done in stage_norm.get(n, []):
-                soft_norm(done)
-        for n in (n_groups, n_groups + 1):
-            for done in stage_norm.get(n, []):
-                soft_norm(done)
-            for done in stage_max.get(n, []):
+                    multiply(open_q[(c, gp)], u, h0, nh)
+            for done in stage_max.get(u, []):
                 soft_max(done)
                 soft_exp(done)
+            for done in stage_norm.get(u, []):
+                soft_norm(done)
+            if ten == 0:
+                open_q[(c, gp)] = u
+            elif c == CB - 1:
+                stage_max[u + 1] = [gp]
+                stage_norm[u + 2] = [gp]
+        for u in (n_steps, n_steps + 1):
+            for done in stage_max.get(u, []):
+                soft_max(done)
+                soft_exp(done)
+            for done in stage_norm.get(u, []):
+                soft_norm(done)

@@ -16,13 +16,17 @@ S = 16384
 H = 8
 DH = 64
 G = 8
-CB = 4
-UNIT = H * DH
-SCALE = 0.125
-GC = 4
-RAW_BUFS = 8
-SPLIT_STEPS = 2
-PIECES = 4
+J_RANGES = S // G // (P * PACK)
+G_COLS = H * DH
+PAIR_COLS = 2 * DH
+SCALE = DH**-0.5
+G_PER_LOAD = (4, 4, 2, 2)
+RUN = 4
+RAW_BUFS = 6
+GROUPED_BUFS = 3
+WORD_BUFS = 6
+SOFTMAX_BUFS = 4
+CUT_H = 2
 
 FLOPS = 2 * G * DH * DH * S
 BYTES = 2 * S * H * DH * 2 + G * DH * DH * 4
@@ -31,144 +35,166 @@ BYTES = 2 * S * H * DH * 2 + G * DH * DH * 4
 def tile_flaxattention2_kernel(tc, query, key, value, out):
     nc = tc.nc
     pattern = "b (c p t g) h d -> (b c) p t (g h d)"
-    views = [x.rearrange(pattern, c=CB, p=P, t=PACK, g=G) for x in (query, key)]
+    views = [x.rearrange(pattern, c=J_RANGES, p=P, t=PACK, g=G) for x in (query, key)]
     out_rows = out.rearrange("g d e -> (g d) e")
 
-    chunks = [(ten, c, part) for c in range(CB) for part in range(G // GC) for ten in range(2)]
+    loads = [
+        (tensor, c, g0, G_PER_LOAD[c])
+        for c in range(J_RANGES)
+        for g0 in range(0, G, G_PER_LOAD[c])
+        for tensor in range(2)
+    ]
     steps = []
-    for k, (ten, c, part) in enumerate(chunks):
-        for pl in range(GC // 2):
-            steps.append((ten, c, part * (GC // 2) + pl, k, pl))
+    for k, (tensor, c, g0, n_g) in enumerate(loads):
+        for place in range(n_g // 2):
+            steps.append((tensor, c, g0 // 2 + place, k, place))
     n_steps = len(steps)
 
     with ExitStack() as ctx:
-        raw_pool = ctx.enter_context(tc.tile_pool(name="raw", bufs=RAW_BUFS))
-        grp_pool = ctx.enter_context(tc.tile_pool(name="grp", bufs=3))
-        wrd_pool = ctx.enter_context(tc.tile_pool(name="wrd", bufs=6))
+        raw_pools = {
+            n_g: ctx.enter_context(tc.tile_pool(name="raw%d" % n_g, bufs=RAW_BUFS)) for n_g in sorted(set(G_PER_LOAD))
+        }
+        grp_pool = ctx.enter_context(tc.tile_pool(name="grp", bufs=GROUPED_BUFS))
+        wrd_pool = ctx.enter_context(tc.tile_pool(name="wrd", bufs=WORD_BUFS))
         small = ctx.enter_context(tc.tile_pool(name="small", bufs=1))
-        soft = ctx.enter_context(tc.tile_pool(name="soft", bufs=4))
+        soft = ctx.enter_context(tc.tile_pool(name="soft", bufs=SOFTMAX_BUFS))
         psum = ctx.enter_context(tc.psum_pool(name="acc", bufs=1))
         ctx.enter_context(tc.manual_schedule())
 
-        acc = [psum.tile([P, 2 * DH], F32, name="acc%d" % gp) for gp in range(G // 2)]
+        acc = [psum.tile([P, PAIR_COLS], F32, name="acc%d" % pair) for pair in range(G // 2)]
         raws = {}
         grouped = {}
         words = {}
         planes = {}
         soft_tiles = {}
 
-        def load(k):
-            ten, c, part = chunks[k]
-            raw = raw_pool.tile([P, PACK, GC * UNIT], BF16, name="raw")
-            nc.sync.dma_start(out=raw[:], in_=views[ten][c][:, :, part * GC * UNIT : (part + 1) * GC * UNIT])
-            raws[k] = raw
+        written = {"loads": 0}
+        held = {n_g: 0 for n_g in raw_pools}
+
+        def write_loads():
+            while written["loads"] < len(loads) and held[loads[written["loads"]][3]] < RAW_BUFS:
+                k = written["loads"]
+                tensor, c, g0, n_g = loads[k]
+                raw = raw_pools[n_g].tile([P, PACK, n_g * G_COLS], BF16, name="raw")
+                nc.sync.dma_start(out=raw[:], in_=views[tensor][c][:, :, g0 * G_COLS : (g0 + n_g) * G_COLS])
+                raws[k] = raw
+                held[n_g] = held[n_g] + 1
+                written["loads"] = k + 1
 
         def regroup(u):
-            ten, c, gp, k, pl = steps[u]
+            k, place = steps[u][3], steps[u][4]
             grp = grp_pool.tile([P, H, 2, DH, PACK], BF16, name="grp", align_bytes=64)
             grouped[u] = grp
             for g2, copy in ((0, nc.vector.tensor_copy), (1, nc.scalar.copy)):
-                gl = 2 * pl + g2
-                src = raws[k][:, :, gl * UNIT : (gl + 1) * UNIT].rearrange("p t (h c i) -> p h c t i", h=H, i=4)
-                dst = grp[:, :, g2, :, :].rearrange("p h (c i) t -> p h c t i", i=4)
+                g_in_load = 2 * place + g2
+                src = raws[k][:, :, g_in_load * G_COLS : (g_in_load + 1) * G_COLS].rearrange(
+                    "p t (h n i) -> p h n t i", h=H, i=RUN
+                )
+                dst = grp[:, :, g2, :, :].rearrange("p h (n i) t -> p h n t i", i=RUN)
                 copy(out=dst, in_=src)
+            n_g = loads[k][3]
+            if place == n_g // 2 - 1:
+                held[n_g] = held[n_g] - 1
+                write_loads()
 
         def quantise(u, h0, nh):
             if h0 == 0:
-                words[u] = wrd_pool.tile([P, 2 * UNIT], U32, name="wrd", align_bytes=64)
-                planes[u] = wrd_pool.tile([P, 2 * UNIT], U8, name="pln", align_bytes=64)
-            cols = slice(2 * DH * h0, 2 * DH * (h0 + nh))
+                words[u] = wrd_pool.tile([P, H * PAIR_COLS], U32, name="wrd", align_bytes=64)
+                planes[u] = wrd_pool.tile([P, H * PAIR_COLS], U8, name="pln", align_bytes=64)
+            cols = slice(PAIR_COLS * h0, PAIR_COLS * (h0 + nh))
             nc.vector.quantize_mx(
                 out=words[u][:, cols].bitcast(FP8X4),
                 scales=planes[u][:, cols],
                 in_=grouped[u][:, h0 : h0 + nh, :, :, :].rearrange("p h g d t -> p (h g d t)"),
             )
 
-        def multiply(uq, uk, h0, nh):
-            ten, c, gp, k, pl = steps[uk]
+        def multiply(u_query, u_key, h0, nh):
+            c, pair = steps[u_key][1], steps[u_key][2]
             for h in range(h0, h0 + nh):
-                cols = slice(2 * DH * h, 2 * DH * (h + 1))
+                cols = slice(PAIR_COLS * h, PAIR_COLS * (h + 1))
                 nc.tensor.matmul_mx(
-                    out=acc[gp][:],
-                    lhsT=words[uq][:, cols].bitcast(FP8X4),
-                    lhsT_scale=planes[uq][:, cols],
-                    rhs=words[uk][:, cols].bitcast(FP8X4),
-                    rhs_scale=planes[uk][:, cols],
+                    out=acc[pair][:],
+                    lhsT=words[u_query][:, cols].bitcast(FP8X4),
+                    lhsT_scale=planes[u_query][:, cols],
+                    rhs=words[u_key][:, cols].bitcast(FP8X4),
+                    rhs_scale=planes[u_key][:, cols],
                     start=(c == 0 and h == 0),
-                    stop=(c == CB - 1 and h == H - 1),
+                    stop=(c == J_RANGES - 1 and h == H - 1),
                 )
 
-        def soft_max(gp):
+        def soft_max(pair):
             top = soft.tile([P, 1], F32, name="top")
             shift = soft.tile([P, 1], F32, name="shift")
             for g2 in range(2):
-                rows = slice(DH * g2, DH * (g2 + 1))
-                nc.vector.reduce_max(out=top[rows, :], in_=acc[gp][rows, rows], axis=AX)
+                own = slice(DH * g2, DH * (g2 + 1))
+                nc.vector.reduce_max(out=top[own, :], in_=acc[pair][own, own], axis=AX)
             nc.vector.tensor_scalar_mul(out=shift[:], in0=top[:], scalar1=-SCALE)
-            soft_tiles[gp] = [shift]
+            soft_tiles[pair] = [shift]
 
-        def soft_exp(gp):
-            shift = soft_tiles[gp][0]
+        def soft_exp(pair):
+            shift = soft_tiles[pair][0]
             expo = soft.tile([P, DH], F32, name="expo")
             total = soft.tile([P, 1], F32, name="total")
             for g2 in range(2):
-                rows = slice(DH * g2, DH * (g2 + 1))
+                own = slice(DH * g2, DH * (g2 + 1))
                 nc.scalar.activation(
-                    out=expo[rows, :],
-                    in_=acc[gp][rows, rows],
+                    out=expo[own, :],
+                    in_=acc[pair][own, own],
                     func=EXP,
-                    bias=shift[rows, :],
+                    bias=shift[own, :],
                     scale=SCALE,
-                    accum_out=total[rows, :],
+                    accum_out=total[own, :],
                 )
-            soft_tiles[gp] = [expo, total]
+            soft_tiles[pair] = [expo, total]
 
-        def soft_norm(gp):
-            expo, total = soft_tiles[gp]
+        def soft_norm(pair):
+            expo, total = soft_tiles[pair]
             inv = soft.tile([P, 1], F32, name="inv")
             prob = soft.tile([P, DH], F32, name="prob")
             nc.vector.reciprocal(out=inv[:], in_=total[:])
             nc.vector.tensor_scalar_mul(out=prob[:], in0=expo[:], scalar1=inv[:, 0:1])
-            nc.sync.dma_start(out=out_rows[P * gp : P * (gp + 1), :], in_=prob[:])
+            nc.sync.dma_start(out=out_rows[P * pair : P * (pair + 1), :], in_=prob[:])
 
         warm_in = small.tile([P, 1], F32, name="warm_in")
         warm_out = small.tile([P, 1], F32, name="warm_out")
         nc.vector.memset(warm_in[:], 0.0)
         nc.scalar.activation(out=warm_out[:], in_=warm_in[:], func=EXP)
 
-        for k in range(min(RAW_BUFS, len(chunks))):
-            load(k)
+        write_loads()
 
-        open_q = {}
-        stage_max = {}
-        stage_norm = {}
+        query_step = {}
+        max_due = {}
+        exp_due = []
+        norm_due = []
         regroup(0)
         for u in range(n_steps):
-            ten, c, gp, k, pl = steps[u]
+            tensor, c, pair = steps[u][0], steps[u][1], steps[u][2]
             if u + 1 < n_steps:
                 regroup(u + 1)
-                k_next = steps[u + 1][3]
-                last_of_chunk = u + 2 >= n_steps or steps[u + 2][3] != k_next
-                if last_of_chunk and k_next + RAW_BUFS < len(chunks):
-                    load(k_next + RAW_BUFS)
-            nh = H // PIECES if u >= n_steps - SPLIT_STEPS else H
+            copies_written = u + 1 >= n_steps - 1
+            if copies_written:
+                for due in exp_due:
+                    soft_exp(due)
+                norm_due.extend(exp_due)
+                exp_due = []
+            nh = CUT_H if u == n_steps - 1 else H
             for h0 in range(0, H, nh):
                 quantise(u, h0, nh)
-                if ten == 1:
-                    multiply(open_q[(c, gp)], u, h0, nh)
-            for done in stage_max.get(u, []):
-                soft_max(done)
-                soft_exp(done)
-            for done in stage_norm.get(u, []):
-                soft_norm(done)
-            if ten == 0:
-                open_q[(c, gp)] = u
-            elif c == CB - 1:
-                stage_max[u + 1] = [gp]
-                stage_norm[u + 2] = [gp]
-        for u in (n_steps, n_steps + 1):
-            for done in stage_max.get(u, []):
-                soft_max(done)
-                soft_exp(done)
-            for done in stage_norm.get(u, []):
-                soft_norm(done)
+                if tensor == 1:
+                    multiply(query_step[(c, pair)], u, h0, nh)
+            if u in max_due:
+                soft_max(max_due[u])
+                exp_due.append(max_due[u])
+            if tensor == 0:
+                query_step[(c, pair)] = u
+            elif c == J_RANGES - 1:
+                max_due[u + 1] = pair
+        for due in exp_due:
+            soft_exp(due)
+        norm_due.extend(exp_due)
+        soft_norm(norm_due[0])
+        soft_max(max_due[n_steps])
+        soft_exp(max_due[n_steps])
+        for due in norm_due[1:]:
+            soft_norm(due)
+        soft_norm(max_due[n_steps])

@@ -23,7 +23,9 @@ SCALE = DH**-0.5
 G_PER_LOAD = (4, 4, 2, 2)
 RUN = 4
 RAW_BUFS = 6
-GROUPED_BUFS = 3
+GROUPED_BUFS = 4
+SHIFT_EVERY = 4
+SHIFT_H = 2
 WORD_BUFS = 6
 SOFTMAX_BUFS = 4
 CUT_H = 2
@@ -85,12 +87,16 @@ def tile_flaxattention2_kernel(tc, query, key, value, out):
             k, place = steps[u][3], steps[u][4]
             grp = grp_pool.tile([P, H, 2, DH, PACK], BF16, name="grp", align_bytes=64)
             grouped[u] = grp
-            for g2, copy in ((0, nc.vector.tensor_copy), (1, nc.scalar.copy)):
-                g_in_load = 2 * place + g2
-                src = raws[k][:, :, g_in_load * G_COLS : (g_in_load + 1) * G_COLS].rearrange(
-                    "p t (h n i) -> p h n t i", h=H, i=RUN
+            shifted = SHIFT_H if u % SHIFT_EVERY == SHIFT_EVERY - 1 else 0
+            shares = [(0, 0, H, nc.vector.tensor_copy), (1, 0, H - shifted, nc.scalar.copy)]
+            if shifted:
+                shares.append((1, H - shifted, H, nc.vector.tensor_copy))
+            for g2, h0, h1, copy in shares:
+                col0 = (2 * place + g2) * G_COLS
+                src = raws[k][:, :, col0 + h0 * DH : col0 + h1 * DH].rearrange(
+                    "p t (h n i) -> p h n t i", h=h1 - h0, i=RUN
                 )
-                dst = grp[:, :, g2, :, :].rearrange("p h (n i) t -> p h n t i", i=RUN)
+                dst = grp[:, h0:h1, g2, :, :].rearrange("p h (n i) t -> p h n t i", i=RUN)
                 copy(out=dst, in_=src)
             n_g = loads[k][3]
             if place == n_g // 2 - 1:

@@ -88,9 +88,9 @@ def tile_flaxattention2_kernel(tc, query, key, value, out):
             grp = grp_pool.tile([P, H, 2, DH, PACK], BF16, name="grp", align_bytes=64)
             grouped[u] = grp
             shifted = SHIFT_H if u % SHIFT_EVERY == SHIFT_EVERY - 1 else 0
-            shares = [(0, 0, H, nc.vector.tensor_copy), (1, 0, H - shifted, nc.scalar.copy)]
+            shares = [(0, 0, H - shifted, nc.vector.tensor_copy), (1, 0, H, nc.scalar.copy)]
             if shifted:
-                shares.append((1, H - shifted, H, nc.vector.tensor_copy))
+                shares.append((0, H - shifted, H, nc.scalar.copy))
             for g2, h0, h1, copy in shares:
                 col0 = (2 * place + g2) * G_COLS
                 src = raws[k][:, :, col0 + h0 * DH : col0 + h1 * DH].rearrange(

@@ -21,7 +21,8 @@ G_COLS = H * DH
 PAIR_COLS = 2 * DH
 SCALE = DH**-0.5
 G_PER_LOAD = (4, 4, 2, 2)
-RUN = 4
+RUN_VECTOR = 2
+RUN_SCALAR = 8
 RAW_BUFS = 6
 GROUPED_BUFS = 4
 SHIFT_EVERY = 4
@@ -88,15 +89,15 @@ def tile_flaxattention2_kernel(tc, query, key, value, out):
             grp = grp_pool.tile([P, H, 2, DH, PACK], BF16, name="grp", align_bytes=64)
             grouped[u] = grp
             shifted = SHIFT_H if u % SHIFT_EVERY == SHIFT_EVERY - 1 else 0
-            shares = [(0, 0, H - shifted, nc.vector.tensor_copy), (1, 0, H, nc.scalar.copy)]
+            shares = [(0, 0, H - shifted, nc.vector.tensor_copy, RUN_VECTOR), (1, 0, H, nc.scalar.copy, RUN_SCALAR)]
             if shifted:
-                shares.append((0, H - shifted, H, nc.scalar.copy))
-            for g2, h0, h1, copy in shares:
+                shares.append((0, H - shifted, H, nc.scalar.copy, RUN_SCALAR))
+            for g2, h0, h1, copy, run in shares:
                 col0 = (2 * place + g2) * G_COLS
                 src = raws[k][:, :, col0 + h0 * DH : col0 + h1 * DH].rearrange(
-                    "p t (h n i) -> p h n t i", h=h1 - h0, i=RUN
+                    "p t (h n i) -> p h n t i", h=h1 - h0, i=run
                 )
-                dst = grp[:, h0:h1, g2, :, :].rearrange("p h (n i) t -> p h n t i", i=RUN)
+                dst = grp[:, h0:h1, g2, :, :].rearrange("p h (n i) t -> p h n t i", i=run)
                 copy(out=dst, in_=src)
             n_g = loads[k][3]
             if place == n_g // 2 - 1:

from contextlib import ExitStack

import concourse.mybir as mybir

BF16 = mybir.dt.bfloat16
F32 = mybir.dt.float32
U32 = mybir.dt.uint32
U8 = mybir.dt.uint8
FP8X4 = mybir.dt.float8_e4m3fn_x4
EXP = mybir.ActivationFunctionType.Exp
AX = mybir.AxisListType.X

P = 128
PACK = 4
S = 16384
H = 8
DH = 64
G = 8
J_RANGES = S // G // (P * PACK)
G_COLS = H * DH
PAIR_COLS = 2 * DH
SCALE = DH**-0.5
G_PER_LOAD = (4, 4, 2, 2)
RUN_VECTOR = 2
RUN_SCALAR = 8
RAW_BUFS = 6
GROUPED_BUFS = 4
SHIFT_EVERY = 4
SHIFT_H = 2
WORD_BUFS = 6
SOFTMAX_BUFS = 4
CUT_H = 2

FLOPS = 2 * G * DH * DH * S
BYTES = 2 * S * H * DH * 2 + G * DH * DH * 4


def tile_flaxattention2_kernel(tc, query, key, value, out):
    nc = tc.nc
    pattern = "b (c p t g) h d -> (b c) p t (g h d)"
    views = [x.rearrange(pattern, c=J_RANGES, p=P, t=PACK, g=G) for x in (query, key)]
    out_rows = out.rearrange("g d e -> (g d) e")

    loads = [
        (tensor, c, g0, G_PER_LOAD[c])
        for c in range(J_RANGES)
        for g0 in range(0, G, G_PER_LOAD[c])
        for tensor in range(2)
    ]
    steps = []
    for k, (tensor, c, g0, n_g) in enumerate(loads):
        for place in range(n_g // 2):
            steps.append((tensor, c, g0 // 2 + place, k, place))
    n_steps = len(steps)

    with ExitStack() as ctx:
        raw_pools = {
            n_g: ctx.enter_context(tc.tile_pool(name="raw%d" % n_g, bufs=RAW_BUFS)) for n_g in sorted(set(G_PER_LOAD))
        }
        grp_pool = ctx.enter_context(tc.tile_pool(name="grp", bufs=GROUPED_BUFS))
        wrd_pool = ctx.enter_context(tc.tile_pool(name="wrd", bufs=WORD_BUFS))
        small = ctx.enter_context(tc.tile_pool(name="small", bufs=1))
        soft = ctx.enter_context(tc.tile_pool(name="soft", bufs=SOFTMAX_BUFS))
        psum = ctx.enter_context(tc.psum_pool(name="acc", bufs=1))
        ctx.enter_context(tc.manual_schedule())

        acc = [psum.tile([P, PAIR_COLS], F32, name="acc%d" % pair) for pair in range(G // 2)]
        raws = {}
        grouped = {}
        words = {}
        planes = {}
        soft_tiles = {}

        written = {"loads": 0}
        held = {n_g: 0 for n_g in raw_pools}

        def write_loads():
            while written["loads"] < len(loads) and held[loads[written["loads"]][3]] < RAW_BUFS:
                k = written["loads"]
                tensor, c, g0, n_g = loads[k]
                raw = raw_pools[n_g].tile([P, PACK, n_g * G_COLS], BF16, name="raw")
                nc.sync.dma_start(out=raw[:], in_=views[tensor][c][:, :, g0 * G_COLS : (g0 + n_g) * G_COLS])
                raws[k] = raw
                held[n_g] = held[n_g] + 1
                written["loads"] = k + 1

        def regroup(u):
            k, place = steps[u][3], steps[u][4]
            grp = grp_pool.tile([P, H, 2, DH, PACK], BF16, name="grp", align_bytes=64)
            grouped[u] = grp
            shifted = SHIFT_H if u % SHIFT_EVERY == SHIFT_EVERY - 1 else 0
            shares = [(0, 0, H - shifted, nc.vector.tensor_copy, RUN_VECTOR), (1, 0, H, nc.scalar.copy, RUN_SCALAR)]
            if shifted:
                shares.append((0, H - shifted, H, nc.scalar.copy, RUN_SCALAR))
            for g2, h0, h1, copy, run in shares:
                col0 = (2 * place + g2) * G_COLS
                src = raws[k][:, :, col0 + h0 * DH : col0 + h1 * DH].rearrange(
                    "p t (h n i) -> p h n t i", h=h1 - h0, i=run
                )
                dst = grp[:, h0:h1, g2, :, :].rearrange("p h (n i) t -> p h n t i", i=run)
                copy(out=dst, in_=src)
            n_g = loads[k][3]
            if place == n_g // 2 - 1:
                held[n_g] = held[n_g] - 1
                write_loads()

        def quantise(u, h0, nh):
            if h0 == 0:
                words[u] = wrd_pool.tile([P, H * PAIR_COLS], U32, name="wrd", align_bytes=64)
                planes[u] = wrd_pool.tile([P, H * PAIR_COLS], U8, name="pln", align_bytes=64)
            cols = slice(PAIR_COLS * h0, PAIR_COLS * (h0 + nh))
            nc.vector.quantize_mx(
                out=words[u][:, cols].bitcast(FP8X4),
                scales=planes[u][:, cols],
                in_=grouped[u][:, h0 : h0 + nh, :, :, :].rearrange("p h g d t -> p (h g d t)"),
            )

        def multiply(u_query, u_key, h0, nh):
            c, pair = steps[u_key][1], steps[u_key][2]
            for h in range(h0, h0 + nh):
                cols = slice(PAIR_COLS * h, PAIR_COLS * (h + 1))
                nc.tensor.matmul_mx(
                    out=acc[pair][:],
                    lhsT=words[u_query][:, cols].bitcast(FP8X4),
                    lhsT_scale=planes[u_query][:, cols],
                    rhs=words[u_key][:, cols].bitcast(FP8X4),
                    rhs_scale=planes[u_key][:, cols],
                    start=(c == 0 and h == 0),
                    stop=(c == J_RANGES - 1 and h == H - 1),
                )

        def soft_max(pair):
            top = soft.tile([P, 1], F32, name="top")
            shift = soft.tile([P, 1], F32, name="shift")
            for g2 in range(2):
                own = slice(DH * g2, DH * (g2 + 1))
                nc.vector.reduce_max(out=top[own, :], in_=acc[pair][own, own], axis=AX)
            nc.vector.tensor_scalar_mul(out=shift[:], in0=top[:], scalar1=-SCALE)
            soft_tiles[pair] = [shift]

        def soft_exp(pair):
            shift = soft_tiles[pair][0]
            expo = soft.tile([P, DH], F32, name="expo")
            total = soft.tile([P, 1], F32, name="total")
            for g2 in range(2):
                own = slice(DH * g2, DH * (g2 + 1))
                nc.scalar.activation(
                    out=expo[own, :],
                    in_=acc[pair][own, own],
                    func=EXP,
                    bias=shift[own, :],
                    scale=SCALE,
                    accum_out=total[own, :],
                )
            soft_tiles[pair] = [expo, total]

        def soft_norm(pair):
            expo, total = soft_tiles[pair]
            inv = soft.tile([P, 1], F32, name="inv")
            prob = soft.tile([P, DH], F32, name="prob")
            nc.vector.reciprocal(out=inv[:], in_=total[:])
            nc.vector.tensor_scalar_mul(out=prob[:], in0=expo[:], scalar1=inv[:, 0:1])
            nc.sync.dma_start(out=out_rows[P * pair : P * (pair + 1), :], in_=prob[:])

        warm_in = small.tile([P, 1], F32, name="warm_in")
        warm_out = small.tile([P, 1], F32, name="warm_out")
        nc.vector.memset(warm_in[:], 0.0)
        nc.scalar.activation(out=warm_out[:], in_=warm_in[:], func=EXP)

        write_loads()

        query_step = {}
        max_due = {}
        exp_due = []
        norm_due = []
        regroup(0)
        for u in range(n_steps):
            tensor, c, pair = steps[u][0], steps[u][1], steps[u][2]
            if u + 1 < n_steps:
                regroup(u + 1)
            copies_written = u + 1 >= n_steps - 1
            if copies_written:
                for due in exp_due:
                    soft_exp(due)
                norm_due.extend(exp_due)
                exp_due = []
            nh = CUT_H if u == n_steps - 1 else H
            for h0 in range(0, H, nh):
                quantise(u, h0, nh)
                if tensor == 1:
                    multiply(query_step[(c, pair)], u, h0, nh)
            if u in max_due:
                soft_max(max_due[u])
                exp_due.append(max_due[u])
            if tensor == 0:
                query_step[(c, pair)] = u
            elif c == J_RANGES - 1:
                max_due[u + 1] = pair
        for due in exp_due:
            soft_exp(due)
        norm_due.extend(exp_due)
        soft_norm(norm_due[0])
        soft_max(max_due[n_steps])
        soft_exp(max_due[n_steps])
        for due in norm_due[1:]:
            soft_norm(due)
        soft_norm(max_due[n_steps])
